import numpy as np
import ml_dtypes


def mxq(x, axis, fmt="e4m3"):
    dtype, down = {"e4m3": (ml_dtypes.float8_e4m3fn, 7), "e5m2": (ml_dtypes.float8_e5m2, 14)}[fmt]
    v = np.moveaxis(np.asarray(x, np.float32).astype(ml_dtypes.bfloat16).astype(np.float64), axis, -1)
    blocks = v.reshape(v.shape[:-1] + (-1, 32))
    amax = np.abs(blocks).max(-1, keepdims=True)
    byte = np.maximum(np.where(amax > 0, np.frexp(amax)[1] - 1 + 127, 0) - down, 1)
    scale = np.exp2(byte - 127.0)
    codes = (blocks / scale).astype(np.float32).astype(dtype).astype(np.float64)
    return np.moveaxis((codes * scale).reshape(v.shape), -1, axis)


WIDE = False


def mx_kscale(k):
    if not WIDE:
        return np.ones(k)
    levels = np.array([10, -10, 5, -5, 0])
    if k % 512:
        return np.exp2(np.random.permutation(np.resize(levels, k // 32))).repeat(32)
    a = np.empty((k // 512, 16))
    for p in range(k // 512):
        a[p, :8] = np.random.permutation(np.resize(levels, 8))
        for g in range(8):
            far = levels[np.abs(levels - a[p, g]) >= 10]
            a[p, g + 8] = far[np.random.randint(len(far))]
    return np.exp2(a.ravel()).repeat(32)


BF16 = ml_dtypes.bfloat16


def bf(x):
    return np.asarray(x, np.float32).astype(BF16)


def f64(x):
    return np.asarray(x).astype(np.float64)


B, N, HD, NH, KVH, D = 1, 512, 2048, 16, 4, 128
QD = NH * D
KVD = KVH * D
EPS = 2.0 ** -23


def setup_inputs():
    s = mx_kscale(HD)
    rows = np.exp2(np.random.uniform(-2.0, 2.0, (B, N, 1)))
    rows = np.where(np.random.random((B, N, 1)) < 0.125, rows * 2.0 ** -11, rows)
    return {"tokens": bf(np.random.standard_normal((B, N, HD)) * rows),
            "norm_w": bf((1.0 + 0.1 * np.random.standard_normal(HD)) * s),
            "Wq": bf(np.random.standard_normal((QD, HD)) * 0.4 / np.sqrt(HD) / s[None, :]),
            "bq": bf(np.random.standard_normal(QD) * 0.1),
            "Wk": bf(np.random.standard_normal((KVD, HD)) * 0.4 / np.sqrt(HD) / s[None, :]),
            "bk": bf(np.random.standard_normal(KVD) * 0.1),
            "Wv": bf(np.random.standard_normal((KVD, HD)) / np.sqrt(HD) / s[None, :]),
            "bv": bf(np.random.standard_normal(KVD) * 0.3)}


def reference(tokens, norm_w, Wq, bq, Wk, bk, Wv, bv):
    t = f64(tokens)
    x = t / np.sqrt(np.mean(t * t, axis=-1, keepdims=True) + EPS) * f64(norm_w)
    xq = mxq(x, 2, "e4m3")
    q = ((xq @ mxq(f64(Wq), 1, "e4m3").T) + f64(bq)).reshape(B, N, NH, D).transpose(0, 2, 1, 3)
    k = ((xq @ mxq(f64(Wk), 1, "e4m3").T) + f64(bk)).reshape(B, N, KVH, D).transpose(0, 2, 1, 3)
    v = ((xq @ mxq(f64(Wv), 1, "e4m3").T) + f64(bv)).reshape(B, N, KVH, D).transpose(0, 2, 1, 3)
    return q, k, v

@@ -1,0 +1,261 @@
+from contextlib import ExitStack
+
+import concourse.mybir as mybir
+from concourse.masks import make_identity
+
+F32 = mybir.dt.float32
+BF16 = mybir.dt.bfloat16
+I32 = mybir.dt.int32
+U32 = mybir.dt.uint32
+U8 = mybir.dt.uint8
+FP8X4 = mybir.dt.float8_e4m3fn_x4
+ACT = mybir.ActivationFunctionType
+ALU = mybir.AluOpType
+
+P = 128
+PACK = 4
+K_PASS = P * PACK
+N_TOK = 512
+HD = 2048
+PASSES = HD // K_PASS
+TOK_TILES = N_TOK // P
+GROUP = 512
+HEADS = GROUP // P
+Q_GROUPS = 4
+GROUPS = Q_GROUPS + 2
+RAW_GROUPS = 3
+EPS = 2.0 ** -23
+
+FLOPS = 2 * N_TOK * GROUPS * GROUP * HD
+
+
+def tile_attentionlayerdecoder_pa_kernel(
+    tc, tokens, norm_w, Wq, bq, Wk, bk, Wv, bv, out_0, out_1, out_2
+):
+    nc = tc.nc
+    token_rows = tokens.rearrange("b n k -> (b n) k")
+    q_heads = out_0.rearrange("b h n d -> (b h) n d")
+
+    group_rows = [Wq[q * GROUP : (q + 1) * GROUP, :] for q in range(Q_GROUPS)] + [Wk, Wv]
+    group_heads = [q_heads[q * HEADS : (q + 1) * HEADS, :, :] for q in range(Q_GROUPS)] + [
+        out_1.rearrange("b h n d -> (b h) n d"),
+        out_2.rearrange("b h n d -> (b h) n d"),
+    ]
+
+    with ExitStack() as ctx:
+        keep = ctx.enter_context(tc.tile_pool(name="keep", bufs=1))
+        raw_pool = ctx.enter_context(tc.tile_pool(name="raw", bufs=RAW_GROUPS * HEADS))
+        stats = ctx.enter_context(tc.tile_pool(name="stats", bufs=TOK_TILES))
+        rows_pool = ctx.enter_context(tc.tile_pool(name="rows", bufs=2))
+        grouped_pool = ctx.enter_context(tc.tile_pool(name="grouped", bufs=PASSES))
+        result_pool = ctx.enter_context(tc.tile_pool(name="result", bufs=8))
+        psum = ctx.enter_context(tc.psum_pool(name="psum", bufs=8))
+        ctx.enter_context(tc.manual_schedule())
+
+        gain_row = keep.tile([P, HD], BF16)
+        nc.vector.memset(gain_row[:].bitcast(I32), 0)
+        ones = keep.tile([P, P], BF16)
+        nc.vector.memset(ones[:], 1.0)
+        eps_col = keep.tile([P, 1], F32)
+        nc.vector.memset(eps_col[:], EPS)
+        bias_row = keep.tile([P, GROUPS * GROUP], BF16)
+        nc.vector.memset(bias_row[:].bitcast(I32), 0)
+        ident_bf16 = keep.tile([P, P], BF16)
+        make_identity(nc, ident_bf16[:])
+        ident_f32 = keep.tile([P, P], F32)
+        make_identity(nc, ident_f32[:])
+
+        warm = keep.tile([P, 1], F32)
+        nc.scalar.activation(out=warm[:], in_=eps_col[:], func=ACT.Sqrt)
+
+        def load_gain():
+            nc.sync.dma_start(out=gain_row[0:1, :], in_=norm_w.rearrange("(o k) -> o k", o=1))
+
+        def load_biases():
+            first = 0
+            for bias in (bq, bk, bv):
+                width = bias.shape[0]
+                nc.sync.dma_start(
+                    out=bias_row[0:1, first : first + width],
+                    in_=bias.rearrange("(o c) -> o c", o=1),
+                )
+                first += width
+
+        gain_all = keep.tile([P, HD], BF16)
+        bias_all = keep.tile([P, GROUPS * GROUP], F32)
+        x_codes = keep.tile([P, TOK_TILES, PASSES, P], U32, align_bytes=64)
+        x_scales = keep.tile([P, TOK_TILES, PASSES, P], U8, align_bytes=64)
+        w_codes = [
+            keep.tile([P, PASSES, GROUP], U32, name="w_codes%d" % j, align_bytes=64)
+            for j in range(GROUPS)
+        ]
+        w_scales = [
+            keep.tile([P, PASSES, GROUP], U8, name="w_scales%d" % j, align_bytes=64)
+            for j in range(GROUPS)
+        ]
+        token_tiles = [keep.tile([P, HD], BF16, name="tokens%d" % i) for i in range(TOK_TILES)]
+        raw_heads = {}
+
+        def load_tokens(i):
+            nc.sync.dma_start(out=token_tiles[i][:], in_=token_rows[i * P : (i + 1) * P, :])
+
+        def load_weights(j):
+            for h in range(HEADS):
+                head = raw_pool.tile([P, HD], BF16, name="raw_head", tag="raw_head")
+                nc.sync.dma_start(out=head[:], in_=group_rows[j][h * P : (h + 1) * P, :])
+                raw_heads[(j, h)] = head
+
+        def broadcast_gain():
+            for c in range(HD // GROUP):
+                cols = slice(c * GROUP, (c + 1) * GROUP)
+                bank = psum.tile([P, GROUP], F32, tag="bank")
+                nc.tensor.matmul(out=bank[:], lhsT=ones[:], rhs=gain_row[:, cols], start=True, stop=True)
+                nc.vector.tensor_copy(out=gain_all[:, cols], in_=bank[:])
+
+        def broadcast_bias(j):
+            cols = slice(j * GROUP, (j + 1) * GROUP)
+            bank = psum.tile([P, GROUP], F32, tag="bank")
+            nc.tensor.matmul(out=bank[:], lhsT=ones[:], rhs=bias_row[:, cols], start=True, stop=True)
+            nc.scalar.copy(out=bias_all[:, cols], in_=bank[:])
+
+        def normalise(i):
+            squares = rows_pool.tile([P, HD], BF16, tag="squares")
+            sum_sq = stats.tile([P, 1], F32, tag="sum_sq")
+            nc.scalar.activation(
+                out=squares[:], in_=token_tiles[i][:], func=ACT.Square, accum_out=sum_sq[:]
+            )
+            rms = stats.tile([P, 1], F32, tag="rms")
+            nc.scalar.activation(
+                out=rms[:], in_=sum_sq[:], func=ACT.Sqrt, scale=1.0 / HD, bias=eps_col[:]
+            )
+            rstd = stats.tile([P, 1], F32, tag="rstd")
+            nc.vector.reciprocal(out=rstd[:], in_=rms[:])
+            x_rows = rows_pool.tile([P, HD], BF16, tag="x_rows")
+            for g in range(PASSES):
+                k_pass = slice(g * K_PASS, (g + 1) * K_PASS)
+                nc.vector.scalar_tensor_tensor(
+                    out=x_rows[:, k_pass].rearrange("n (t p) -> n t p", t=PACK),
+                    in0=token_tiles[i][:, k_pass].rearrange("n (p t) -> n t p", t=PACK),
+                    scalar=rstd[:, 0:1],
+                    in1=gain_all[:, k_pass].rearrange("n (p t) -> n t p", t=PACK),
+                    op0=ALU.mult,
+                    op1=ALU.mult,
+                )
+            return x_rows
+
+        def pack_tokens(i, x_rows):
+            grouped = rows_pool.tile([P, PASSES, P, PACK], BF16, tag="grouped_x", align_bytes=64)
+            for g in range(PASSES):
+                bank = psum.tile([P, PACK, P], BF16, tag="bank")
+                for t in range(PACK):
+                    first = (g * PACK + t) * P
+                    nc.tensor.transpose(
+                        out=bank[:, t, :], in_=x_rows[:, first : first + P], identity=ident_bf16[:]
+                    )
+                copy = nc.scalar.copy if g % 2 == 0 else nc.vector.tensor_copy
+                copy(out=grouped[:, g, :, :], in_=bank[:].rearrange("p t n -> p n t"))
+            nc.vector.quantize_mx(
+                out=x_codes[:, i, :, :].rearrange("p g n -> p (g n)").bitcast(FP8X4),
+                scales=x_scales[:, i, :, :].rearrange("p g n -> p (g n)"),
+                in_=grouped[:].rearrange("p g n t -> p (g n t)"),
+            )
+
+        def transpose_weights(j, g):
+            grouped = grouped_pool.tile([P, GROUP * PACK], BF16, tag="grouped_w", align_bytes=64)
+            words = grouped[:].bitcast(F32).rearrange("p (o u) -> p o u", u=2)
+            for pair in range(HEADS // 2):
+                bank = psum.tile([P, 2, 2 * P], F32, tag="bank")
+                for u in range(2):
+                    words_u = slice(2 * g * P + u, 2 * (g + 1) * P, 2)
+                    for r in range(2):
+                        nc.tensor.transpose(
+                            out=bank[:, u, r * P : (r + 1) * P],
+                            in_=raw_heads[(j, 2 * pair + r)][:].bitcast(F32)[:, words_u],
+                            identity=ident_f32[:],
+                        )
+                nc.scalar.copy(
+                    out=words[:, 2 * pair * P : 2 * (pair + 1) * P, :],
+                    in_=bank[:].rearrange("p u o -> p o u"),
+                )
+            return grouped
+
+        def quantise_weights(j, g, grouped):
+            nc.vector.quantize_mx(
+                out=w_codes[j][:, g, :].bitcast(FP8X4), scales=w_scales[j][:, g, :], in_=grouped[:]
+            )
+
+        def multiply(i, j, store_queue):
+            bank = psum.tile([P, GROUP], F32, tag="bank")
+            for g in range(PASSES):
+                nc.tensor.matmul_mx(
+                    out=bank[:],
+                    lhsT=x_codes[:, i, g, :].bitcast(FP8X4),
+                    lhsT_scale=x_scales[:, i, g, :],
+                    rhs=w_codes[j][:, g, :].bitcast(FP8X4),
+                    rhs_scale=w_scales[j][:, g, :],
+                    start=(g == 0),
+                    stop=(g == PASSES - 1),
+                )
+            result = result_pool.tile([P, GROUP], F32, tag="result")
+            nc.vector.tensor_tensor(
+                out=result[:], in0=bank[:], in1=bias_all[:, j * GROUP : (j + 1) * GROUP], op=ALU.add
+            )
+            store_queue.dma_start(
+                out=group_heads[j][:, i * P : (i + 1) * P, :].rearrange("h n d -> n h d"),
+                in_=result[:].rearrange("n (h d) -> n h d", h=HEADS),
+            )
+
+        def prepare_weights(j, half):
+            passes = (2 * half, 2 * half + 1)
+            grouped = [transpose_weights(j, g) for g in passes]
+            for g, tile_g in zip(passes, grouped):
+                quantise_weights(j, g, tile_g)
+
+        load_gain()
+        load_tokens(0)
+        load_tokens(1)
+        load_biases()
+        load_weights(0)
+        load_weights(1)
+        load_tokens(2)
+        load_weights(2)
+        load_tokens(3)
+
+        broadcast_gain()
+        x_rows_0 = normalise(0)
+        x_rows_1 = normalise(1)
+        pack_tokens(0, x_rows_0)
+        broadcast_bias(0)
+        prepare_weights(0, 0)
+        pack_tokens(1, x_rows_1)
+        prepare_weights(0, 1)
+        load_weights(RAW_GROUPS)
+
+        def lag(i):
+            return 2 * max(0, i - 1)
+
+        late_rows = None
+        for step in range(GROUPS + lag(TOK_TILES - 1)):
+            products = [
+                (i, step - lag(i)) for i in range(TOK_TILES) if 0 <= step - lag(i) < GROUPS
+            ]
+            first_half = (len(products) + 1) // 2
+            preparing = step + 1 < GROUPS
+            store_queue = nc.gpsimd if preparing else nc.sync
+            if preparing:
+                broadcast_bias(step + 1)
+                prepare_weights(step + 1, 0)
+            for i, j in products[:first_half]:
+                multiply(i, j, store_queue)
+            if preparing:
+                prepare_weights(step + 1, 1)
+            for i, j in products[first_half:]:
+                multiply(i, j, store_queue)
+            if step + 1 + RAW_GROUPS < GROUPS:
+                load_weights(step + 1 + RAW_GROUPS)
+            late = 2 + step // 2
+            if late < TOK_TILES:
+                if step % 2 == 0:
+                    late_rows = normalise(late)
+                else:
+                    pack_tokens(late, late_rows)

@@ -19,51 +19,84 @@ N_TOK = 512
 HD = 2048
 PASSES = HD // K_PASS
 TOK_TILES = N_TOK // P
-GROUP = 512
-HEADS = GROUP // P
-Q_GROUPS = 4
-GROUPS = Q_GROUPS + 2
-RAW_GROUPS = 3
+HALVES = HD // 2
+UNIT_HEADS = 2
+UNIT = UNIT_HEADS * P
+UNITS = 12
+OUT = UNITS * UNIT
+PAIRS = TOK_TILES // 2
 EPS = 2.0 ** -23
+RAW_BUFS = 12
+PERM_BUFS = 6
+T_BANKS = 4
+O_BANKS = 4
+BIAS_COLS = 1024
 
-FLOPS = 2 * N_TOK * GROUPS * GROUP * HD
+FLOPS = 2 * N_TOK * OUT * HD
 
 
 def tile_attentionlayerdecoder_pa_kernel(
     tc, tokens, norm_w, Wq, bq, Wk, bk, Wv, bv, out_0, out_1, out_2
 ):
     nc = tc.nc
-    token_rows = tokens.rearrange("b n k -> (b n) k")
-    q_heads = out_0.rearrange("b h n d -> (b h) n d")
+    token_rows = tokens.rearrange("b (p i) k -> (b p) i k", i=TOK_TILES)
 
-    group_rows = [Wq[q * GROUP : (q + 1) * GROUP, :] for q in range(Q_GROUPS)] + [Wk, Wv]
-    group_heads = [q_heads[q * HEADS : (q + 1) * HEADS, :, :] for q in range(Q_GROUPS)] + [
-        out_1.rearrange("b h n d -> (b h) n d"),
-        out_2.rearrange("b h n d -> (b h) n d"),
-    ]
+    head_rows = []
+    head_out = []
+    for w, out in ((Wq, out_0), (Wk, out_1), (Wv, out_2)):
+        for h in range(w.shape[0] // P):
+            head_rows.append(w[h * P : (h + 1) * P, :])
+            head_out.append((out.rearrange("b h n d -> (b h) n d"), h))
 
     with ExitStack() as ctx:
         keep = ctx.enter_context(tc.tile_pool(name="keep", bufs=1))
-        raw_pool = ctx.enter_context(tc.tile_pool(name="raw", bufs=RAW_GROUPS * HEADS))
+        raw_pool = ctx.enter_context(tc.tile_pool(name="raw", bufs=RAW_BUFS))
+        perm_pool = ctx.enter_context(tc.tile_pool(name="perm", bufs=PERM_BUFS))
         stats = ctx.enter_context(tc.tile_pool(name="stats", bufs=TOK_TILES))
         rows_pool = ctx.enter_context(tc.tile_pool(name="rows", bufs=2))
-        grouped_pool = ctx.enter_context(tc.tile_pool(name="grouped", bufs=PASSES))
+        grouped_pool = ctx.enter_context(tc.tile_pool(name="grouped", bufs=4))
         result_pool = ctx.enter_context(tc.tile_pool(name="result", bufs=8))
-        psum = ctx.enter_context(tc.psum_pool(name="psum", bufs=8))
+        t_psum = ctx.enter_context(tc.psum_pool(name="t_psum", bufs=T_BANKS))
+        o_psum = ctx.enter_context(tc.psum_pool(name="o_psum", bufs=O_BANKS))
         ctx.enter_context(tc.manual_schedule())
 
+        token_tiles = [keep.tile([P, HD], BF16, name="tokens%d" % i) for i in range(TOK_TILES)]
+        raw = {}
+        perm = {}
+
+        def load_tokens(i):
+            nc.sync.dma_start(out=token_tiles[i][:], in_=token_rows[:, i, :])
+
+        def load_head(h):
+            tile = raw_pool.tile([P, HD], BF16, name="raw_head", tag="raw_head")
+            nc.sync.dma_start(out=tile[:], in_=head_rows[h])
+            raw[h] = tile
+
+        load_tokens(0)
+
+        eps_col = keep.tile([P, 1], F32)
+        nc.vector.memset(eps_col[:], EPS)
         gain_row = keep.tile([P, HD], BF16)
         nc.vector.memset(gain_row[:].bitcast(I32), 0)
         ones = keep.tile([P, P], BF16)
         nc.vector.memset(ones[:], 1.0)
-        eps_col = keep.tile([P, 1], F32)
-        nc.vector.memset(eps_col[:], EPS)
-        bias_row = keep.tile([P, GROUPS * GROUP], BF16)
+        bias_row = keep.tile([P, OUT], BF16)
         nc.vector.memset(bias_row[:].bitcast(I32), 0)
-        ident_bf16 = keep.tile([P, P], BF16)
-        make_identity(nc, ident_bf16[:])
-        ident_f32 = keep.tile([P, P], F32)
-        make_identity(nc, ident_f32[:])
+        ident = keep.tile([P, P], F32)
+        make_identity(nc, ident[:])
+
+        gain_all = keep.tile([P, HD], BF16)
+        bias_all = keep.tile([P, OUT], BF16)
+        x_codes = keep.tile([P, TOK_TILES, PASSES, P], U32, align_bytes=64)
+        x_scales = keep.tile([P, TOK_TILES, PASSES, P], U8, align_bytes=64)
+        w_codes = [
+            keep.tile([P, PASSES, UNIT], U32, name="w_codes%d" % k, align_bytes=64)
+            for k in range(UNITS)
+        ]
+        w_scales = [
+            keep.tile([P, PASSES, UNIT], U8, name="w_scales%d" % k, align_bytes=64)
+            for k in range(UNITS)
+        ]
 
         warm = keep.tile([P, 1], F32)
         nc.scalar.activation(out=warm[:], in_=eps_col[:], func=ACT.Sqrt)
@@ -81,181 +114,260 @@ def tile_attentionlayerdecoder_pa_kernel(
                 )
                 first += width
 
-        gain_all = keep.tile([P, HD], BF16)
-        bias_all = keep.tile([P, GROUPS * GROUP], F32)
-        x_codes = keep.tile([P, TOK_TILES, PASSES, P], U32, align_bytes=64)
-        x_scales = keep.tile([P, TOK_TILES, PASSES, P], U8, align_bytes=64)
-        w_codes = [
-            keep.tile([P, PASSES, GROUP], U32, name="w_codes%d" % j, align_bytes=64)
-            for j in range(GROUPS)
-        ]
-        w_scales = [
-            keep.tile([P, PASSES, GROUP], U8, name="w_scales%d" % j, align_bytes=64)
-            for j in range(GROUPS)
-        ]
-        token_tiles = [keep.tile([P, HD], BF16, name="tokens%d" % i) for i in range(TOK_TILES)]
-        raw_heads = {}
+        def spread(row, everywhere, copy):
+            for first in range(0, row.shape[1], BIAS_COLS):
+                bank = t_psum.tile([P, BIAS_COLS], BF16, tag="bank")
+                for c in range(0, BIAS_COLS, 512):
+                    nc.tensor.matmul(
+                        out=bank[:, c : c + 512],
+                        lhsT=ones[:],
+                        rhs=row[:, first + c : first + c + 512],
+                        start=True,
+                        stop=True,
+                    )
+                copy(out=everywhere[:, first : first + BIAS_COLS], in_=bank[:])
 
-        def load_tokens(i):
-            nc.sync.dma_start(out=token_tiles[i][:], in_=token_rows[i * P : (i + 1) * P, :])
+        sums = {}
+        roots = {}
+        rstds = {}
 
-        def load_weights(j):
-            for h in range(HEADS):
-                head = raw_pool.tile([P, HD], BF16, name="raw_head", tag="raw_head")
-                nc.sync.dma_start(out=head[:], in_=group_rows[j][h * P : (h + 1) * P, :])
-                raw_heads[(j, h)] = head
-
-        def broadcast_gain():
-            for c in range(HD // GROUP):
-                cols = slice(c * GROUP, (c + 1) * GROUP)
-                bank = psum.tile([P, GROUP], F32, tag="bank")
-                nc.tensor.matmul(out=bank[:], lhsT=ones[:], rhs=gain_row[:, cols], start=True, stop=True)
-                nc.vector.tensor_copy(out=gain_all[:, cols], in_=bank[:])
-
-        def broadcast_bias(j):
-            cols = slice(j * GROUP, (j + 1) * GROUP)
-            bank = psum.tile([P, GROUP], F32, tag="bank")
-            nc.tensor.matmul(out=bank[:], lhsT=ones[:], rhs=bias_row[:, cols], start=True, stop=True)
-            nc.scalar.copy(out=bias_all[:, cols], in_=bank[:])
-
-        def normalise(i):
+        def square(i):
             squares = rows_pool.tile([P, HD], BF16, tag="squares")
-            sum_sq = stats.tile([P, 1], F32, tag="sum_sq")
+            sums[i] = stats.tile([P, 1], F32, name="sum_sq", tag="sum_sq")
             nc.scalar.activation(
-                out=squares[:], in_=token_tiles[i][:], func=ACT.Square, accum_out=sum_sq[:]
+                out=squares[:], in_=token_tiles[i][:], func=ACT.Square, accum_out=sums[i][:]
             )
-            rms = stats.tile([P, 1], F32, tag="rms")
+
+        def root(i):
+            roots[i] = stats.tile([P, 1], F32, name="rms", tag="rms")
             nc.scalar.activation(
-                out=rms[:], in_=sum_sq[:], func=ACT.Sqrt, scale=1.0 / HD, bias=eps_col[:]
+                out=roots[i][:], in_=sums[i][:], func=ACT.Sqrt, scale=1.0 / HD, bias=eps_col[:]
             )
-            rstd = stats.tile([P, 1], F32, tag="rstd")
-            nc.vector.reciprocal(out=rstd[:], in_=rms[:])
-            x_rows = rows_pool.tile([P, HD], BF16, tag="x_rows")
-            for g in range(PASSES):
-                k_pass = slice(g * K_PASS, (g + 1) * K_PASS)
+
+        x_rows = {}
+
+        def invert(i):
+            rstds[i] = stats.tile([P, 1], F32, name="rstd", tag="rstd")
+            nc.vector.reciprocal(out=rstds[i][:], in_=roots[i][:])
+            x_rows[i] = rows_pool.tile([P, 2, HALVES], BF16, name="x_rows", tag="x_rows")
+
+        def normalise(i, us=(0, 1)):
+            for u in us:
                 nc.vector.scalar_tensor_tensor(
-                    out=x_rows[:, k_pass].rearrange("n (t p) -> n t p", t=PACK),
-                    in0=token_tiles[i][:, k_pass].rearrange("n (p t) -> n t p", t=PACK),
-                    scalar=rstd[:, 0:1],
-                    in1=gain_all[:, k_pass].rearrange("n (p t) -> n t p", t=PACK),
+                    out=x_rows[i][:, u, :].rearrange("n (m e) -> n m e", e=2),
+                    in0=token_tiles[i][:].rearrange("n (m u e) -> n m u e", u=2, e=2)[:, :, u, :],
+                    scalar=rstds[i][:, 0:1],
+                    in1=gain_all[:].rearrange("n (m u e) -> n m u e", u=2, e=2)[:, :, u, :],
                     op0=ALU.mult,
                     op1=ALU.mult,
                 )
-            return x_rows
 
-        def pack_tokens(i, x_rows):
-            grouped = rows_pool.tile([P, PASSES, P, PACK], BF16, tag="grouped_x", align_bytes=64)
-            for g in range(PASSES):
-                bank = psum.tile([P, PACK, P], BF16, tag="bank")
-                for t in range(PACK):
-                    first = (g * PACK + t) * P
-                    nc.tensor.transpose(
-                        out=bank[:, t, :], in_=x_rows[:, first : first + P], identity=ident_bf16[:]
-                    )
-                copy = nc.scalar.copy if g % 2 == 0 else nc.vector.tensor_copy
-                copy(out=grouped[:, g, :, :], in_=bank[:].rearrange("p t n -> p n t"))
+        banks = {}
+
+        def transpose_x(i):
+            words = x_rows[i][:].rearrange("n u k -> n (u k)").bitcast(F32)
+            for half in range(2):
+                bank = t_psum.tile([P, 2, 2, P], F32, tag="bank")
+                for gg in range(2):
+                    for u in range(2):
+                        first = (u * PASSES + 2 * half + gg) * P
+                        nc.tensor.transpose(
+                            out=bank[:, gg, u, :], in_=words[:, first : first + P], identity=ident[:]
+                        )
+                banks[("x", i, half)] = bank
+
+        grouped_x = {}
+
+        def empty_x(i, copy):
+            grouped_x[i] = rows_pool.tile([P, PASSES, P, PACK], BF16, name="grouped_x", tag="grouped_x", align_bytes=64)
+            words = grouped_x[i][:].rearrange("p g n t -> p (g n t)").bitcast(F32)
+            words = words.rearrange("p (g n u) -> p g n u", g=PASSES, u=2)
+            for half in range(2):
+                copy(
+                    out=words[:, 2 * half : 2 * half + 2, :, :],
+                    in_=banks[("x", i, half)][:].rearrange("p g u n -> p g n u"),
+                )
+
+        def quantise_x(i):
             nc.vector.quantize_mx(
                 out=x_codes[:, i, :, :].rearrange("p g n -> p (g n)").bitcast(FP8X4),
                 scales=x_scales[:, i, :, :].rearrange("p g n -> p (g n)"),
-                in_=grouped[:].rearrange("p g n t -> p (g n t)"),
+                in_=grouped_x[i][:].rearrange("p g n t -> p (g n t)"),
             )
 
-        def transpose_weights(j, g):
-            grouped = grouped_pool.tile([P, GROUP * PACK], BF16, tag="grouped_w", align_bytes=64)
-            words = grouped[:].bitcast(F32).rearrange("p (o u) -> p o u", u=2)
-            for pair in range(HEADS // 2):
-                bank = psum.tile([P, 2, 2 * P], F32, tag="bank")
-                for u in range(2):
-                    words_u = slice(2 * g * P + u, 2 * (g + 1) * P, 2)
-                    for r in range(2):
+        def permute(h, copy):
+            perm[h] = perm_pool.tile([P, 2, HALVES], BF16, name="perm_head", tag="perm_head")
+            copy(
+                out=perm[h][:].rearrange("o u k -> o (u k)").bitcast(F32).rearrange("o (u m) -> o u m", u=2),
+                in_=raw[h][:].bitcast(F32).rearrange("o (m u) -> o u m", u=2),
+            )
+
+        def transpose_w(k):
+            for g in range(PASSES):
+                bank = t_psum.tile([P, 2, UNIT], F32, tag="bank")
+                for r in range(UNIT_HEADS):
+                    h = UNIT_HEADS * k + r
+                    for u in range(2):
+                        if h in perm:
+                            first = (u * PASSES + g) * P
+                            words = perm[h][:].rearrange("o u k -> o (u k)").bitcast(F32)
+                            words = words[:, first : first + P]
+                        else:
+                            words = raw[h][:].bitcast(F32)[:, 2 * g * P + u : 2 * (g + 1) * P : 2]
                         nc.tensor.transpose(
                             out=bank[:, u, r * P : (r + 1) * P],
-                            in_=raw_heads[(j, 2 * pair + r)][:].bitcast(F32)[:, words_u],
-                            identity=ident_f32[:],
+                            in_=words,
+                            identity=ident[:],
                         )
-                nc.scalar.copy(
-                    out=words[:, 2 * pair * P : 2 * (pair + 1) * P, :],
-                    in_=bank[:].rearrange("p u o -> p o u"),
-                )
-            return grouped
+                banks[("w", k, g)] = bank
 
-        def quantise_weights(j, g, grouped):
+        grouped_w = {}
+
+        def empty_w(k, g, copy):
+            if g % 2 == 0:
+                grouped_w[(k, g // 2)] = grouped_pool.tile([P, 2, UNIT * PACK], BF16, name="grouped_w", tag="grouped_w", align_bytes=64)
+            words = grouped_w[(k, g // 2)][:].rearrange("p g c -> p (g c)").bitcast(F32)
+            words = words.rearrange("p (g o u) -> p g o u", g=2, u=2)
+            copy(
+                out=words[:, g % 2, :, :],
+                in_=banks[("w", k, g)][:].rearrange("p u o -> p o u"),
+            )
+
+        def quantise_w(k, half):
+            g = slice(2 * half, 2 * half + 2)
             nc.vector.quantize_mx(
-                out=w_codes[j][:, g, :].bitcast(FP8X4), scales=w_scales[j][:, g, :], in_=grouped[:]
+                out=w_codes[k][:, g, :].rearrange("p g o -> p (g o)").bitcast(FP8X4),
+                scales=w_scales[k][:, g, :].rearrange("p g o -> p (g o)"),
+                in_=grouped_w[(k, half)][:].rearrange("p g c -> p (g c)"),
             )
 
-        def multiply(i, j, store_queue):
-            bank = psum.tile([P, GROUP], F32, tag="bank")
-            for g in range(PASSES):
-                nc.tensor.matmul_mx(
-                    out=bank[:],
-                    lhsT=x_codes[:, i, g, :].bitcast(FP8X4),
-                    lhsT_scale=x_scales[:, i, g, :],
-                    rhs=w_codes[j][:, g, :].bitcast(FP8X4),
-                    rhs_scale=w_scales[j][:, g, :],
-                    start=(g == 0),
-                    stop=(g == PASSES - 1),
-                )
-            result = result_pool.tile([P, GROUP], F32, tag="result")
+        def multiply(k, pair, tiles=(0, 1)):
+            if 0 in tiles:
+                banks[("o", k, pair)] = o_psum.tile([P, 2, UNIT], F32, name="out_bank", tag="out")
+            bank = banks[("o", k, pair)]
+            for ii in tiles:
+                i = 2 * pair + ii
+                for g in range(PASSES):
+                    nc.tensor.matmul_mx(
+                        out=bank[:, ii, :],
+                        lhsT=x_codes[:, i, g, :].bitcast(FP8X4),
+                        lhsT_scale=x_scales[:, i, g, :],
+                        rhs=w_codes[k][:, g, :].bitcast(FP8X4),
+                        rhs_scale=w_scales[k][:, g, :],
+                        start=(g == 0),
+                        stop=(g == PASSES - 1),
+                    )
+
+        def finish(k, pair, queue):
+            result = result_pool.tile([P, UNIT_HEADS, 2, P], F32, tag="result")
+            bias = bias_all[:, k * UNIT : (k + 1) * UNIT].rearrange("p (h o d) -> p h o d", h=UNIT_HEADS, o=1)
             nc.vector.tensor_tensor(
-                out=result[:], in0=bank[:], in1=bias_all[:, j * GROUP : (j + 1) * GROUP], op=ALU.add
+                out=result[:],
+                in0=banks[("o", k, pair)][:].rearrange("p i (h d) -> p h i d", h=UNIT_HEADS),
+                in1=bias.to_broadcast([P, UNIT_HEADS, 2, P]),
+                op=ALU.add,
             )
-            store_queue.dma_start(
-                out=group_heads[j][:, i * P : (i + 1) * P, :].rearrange("h n d -> n h d"),
-                in_=result[:].rearrange("n (h d) -> n h d", h=HEADS),
+            out, h = head_out[UNIT_HEADS * k]
+            queue.dma_start(
+                out=out[h : h + UNIT_HEADS, :, :].rearrange("h (p i) d -> p h i d", i=TOK_TILES)[
+                    :, :, 2 * pair : 2 * pair + 2, :
+                ],
+                in_=result[:],
             )
 
-        def prepare_weights(j, half):
-            passes = (2 * half, 2 * half + 1)
-            grouped = [transpose_weights(j, g) for g in passes]
-            for g, tile_g in zip(passes, grouped):
-                quantise_weights(j, g, tile_g)
+        V = nc.vector.tensor_copy
+        S = nc.scalar.copy
 
         load_gain()
-        load_tokens(0)
         load_tokens(1)
+        for h in range(6):
+            load_head(h)
         load_biases()
-        load_weights(0)
-        load_weights(1)
         load_tokens(2)
-        load_weights(2)
+        load_head(6)
+        load_head(7)
         load_tokens(3)
+        for h in range(8, RAW_BUFS):
+            load_head(h)
 
-        broadcast_gain()
-        x_rows_0 = normalise(0)
-        x_rows_1 = normalise(1)
-        pack_tokens(0, x_rows_0)
-        broadcast_bias(0)
-        prepare_weights(0, 0)
-        pack_tokens(1, x_rows_1)
-        prepare_weights(0, 1)
-        load_weights(RAW_GROUPS)
+        NS = 6
+        spread(gain_row, gain_all, V)
+        square(0)
+        root(0)
+        square(1)
+        root(1)
+        transpose_w(0)
+        invert(0)
+        normalise(0)
+        empty_w(0, 0, S)
+        empty_w(0, 1, S)
+        transpose_x(0)
+        invert(1)
+        normalise(1)
+        empty_x(0, S)
+        transpose_w(1)
+        empty_w(0, 2, S)
+        empty_w(0, 3, S)
+        quantise_x(0)
+        quantise_w(0, 0)
+        quantise_w(0, 1)
+        transpose_x(1)
+        empty_x(1, S)
+        multiply(0, 0, (0,))
+        empty_w(1, 0, V)
+        empty_w(1, 1, S)
+        empty_w(1, 2, V)
+        quantise_x(1)
+        empty_w(1, 3, S)
+        spread(bias_row, bias_all, S)
 
-        def lag(i):
-            return 2 * max(0, i - 1)
-
-        late_rows = None
-        for step in range(GROUPS + lag(TOK_TILES - 1)):
-            products = [
-                (i, step - lag(i)) for i in range(TOK_TILES) if 0 <= step - lag(i) < GROUPS
-            ]
-            first_half = (len(products) + 1) // 2
-            preparing = step + 1 < GROUPS
-            store_queue = nc.gpsimd if preparing else nc.sync
-            if preparing:
-                broadcast_bias(step + 1)
-                prepare_weights(step + 1, 0)
-            for i, j in products[:first_half]:
-                multiply(i, j, store_queue)
-            if preparing:
-                prepare_weights(step + 1, 1)
-            for i, j in products[first_half:]:
-                multiply(i, j, store_queue)
-            if step + 1 + RAW_GROUPS < GROUPS:
-                load_weights(step + 1 + RAW_GROUPS)
-            late = 2 + step // 2
-            if late < TOK_TILES:
-                if step % 2 == 0:
-                    late_rows = normalise(late)
-                else:
-                    pack_tokens(late, late_rows)
+        xs = {0: ["sq2"], 1: ["nm2", "sq3"], 2: ["tx2", "nm3"], 3: ["qx2", "tx3"], 4: ["qx3"]}
+        owed = []
+        done = []
+        for k in range(UNITS + 1):
+            if k + 2 < UNITS:
+                transpose_w(k + 2)
+            if k < UNITS:
+                multiply(k, 0, (0, 1) if k else (1,))
+            for kk, pair in done:
+                finish(kk, pair, nc.gpsimd if k < 9 else nc.sync)
+            done = [(k, 0)] if k < UNITS else []
+            owed.append(k)
+            if k + 2 < UNITS:
+                empty_w(k + 2, 0, S)
+                empty_w(k + 2, 1, S)
+            for r in range(UNIT_HEADS):
+                h = UNIT_HEADS * (k + 3) + r
+                if UNIT_HEADS * NS <= h < len(head_rows):
+                    permute(h, V if r == 0 or k < 7 else S)
+                if k + 1 < UNITS:
+                    quantise_w(k + 1, r)
+            if k + 2 < UNITS:
+                empty_w(k + 2, 2, S)
+                empty_w(k + 2, 3, V if k < 0 else S)
+            for st in xs.get(k, []):
+                i = int(st[2])
+                if st[:2] == "sq":
+                    square(i)
+                    root(i)
+                if st[:2] == "nm":
+                    invert(i)
+                    normalise(i)
+                if st[:2] == "tx":
+                    transpose_x(i)
+                    empty_x(i, S)
+                if st[:2] == "qx":
+                    quantise_x(i)
+            if k >= 5:
+                n = 2 if k < UNITS else len(owed)
+                for kk in owed[:n]:
+                    if kk < UNITS:
+                        multiply(kk, 1)
+                        done.append((kk, 1))
+                owed = owed[n:]
+            h = RAW_BUFS + UNIT_HEADS * k
+            for r in range(UNIT_HEADS):
+                if h + r < len(head_rows):
+                    load_head(h + r)
+        for kk, pair in done:
+            finish(kk, pair, nc.sync)

@@ -80,8 +80,6 @@ def tile_attentionlayerdecoder_pa_kernel(
         nc.vector.memset(gain_row[:].bitcast(I32), 0)
         ones = keep.tile([P, P], BF16)
         nc.vector.memset(ones[:], 1.0)
-        bias_row = keep.tile([P, OUT], BF16)
-        nc.vector.memset(bias_row[:].bitcast(I32), 0)
         ident = keep.tile([P, P], F32)
         make_identity(nc, ident[:])
 
@@ -108,10 +106,7 @@ def tile_attentionlayerdecoder_pa_kernel(
             first = 0
             for bias in (bq, bk, bv):
                 width = bias.shape[0]
-                nc.sync.dma_start(
-                    out=bias_row[0:1, first : first + width],
-                    in_=bias.rearrange("(o c) -> o c", o=1),
-                )
+                nc.sync.dma_start(out=bias_all[:, first : first + width], in_=bias.partition_broadcast(P))
                 first += width
 
         def spread(row, everywhere, copy):
@@ -319,7 +314,6 @@ def tile_attentionlayerdecoder_pa_kernel(
         empty_w(1, 2, V)
         quantise_x(1)
         empty_w(1, 3, S)
-        spread(bias_row, bias_all, S)
 
         xs = {0: ["sq2"], 1: ["nm2", "sq3"], 2: ["tx2", "nm3"], 3: ["qx2", "tx3"], 4: ["qx3"]}
         owed = []

@@ -14,23 +14,24 @@ ALU = mybir.AluOpType
 
 P = 128
 PACK = 4
-K_PASS = P * PACK
 N_TOK = 512
 HD = 2048
-PASSES = HD // K_PASS
+PASSES = HD // (P * PACK)
+HALF = PASSES // 2
 TOK_TILES = N_TOK // P
 HALVES = HD // 2
 UNIT_HEADS = 2
 UNIT = UNIT_HEADS * P
 UNITS = 12
 OUT = UNITS * UNIT
-PAIRS = TOK_TILES // 2
 EPS = 2.0 ** -23
 RAW_BUFS = 12
-PERM_BUFS = 6
-T_BANKS = 4
-O_BANKS = 4
-BIAS_COLS = 1024
+PERM_BUFS = 5
+T_BANKS = 5
+O_BANKS = 3
+SPREAD = 1024
+LAG = 5
+FIRST_LAID_OUT = 14
 
 FLOPS = 2 * N_TOK * OUT * HD
 
@@ -47,6 +48,7 @@ def tile_attentionlayerdecoder_pa_kernel(
         for h in range(w.shape[0] // P):
             head_rows.append(w[h * P : (h + 1) * P, :])
             head_out.append((out.rearrange("b h n d -> (b h) n d"), h))
+    n_heads = len(head_rows)
 
     with ExitStack() as ctx:
         keep = ctx.enter_context(tc.tile_pool(name="keep", bufs=1))
@@ -54,11 +56,11 @@ def tile_attentionlayerdecoder_pa_kernel(
         perm_pool = ctx.enter_context(tc.tile_pool(name="perm", bufs=PERM_BUFS))
         stats = ctx.enter_context(tc.tile_pool(name="stats", bufs=TOK_TILES))
         rows_pool = ctx.enter_context(tc.tile_pool(name="rows", bufs=2))
-        grouped_pool = ctx.enter_context(tc.tile_pool(name="grouped", bufs=4))
-        result_pool = ctx.enter_context(tc.tile_pool(name="result", bufs=8))
+        grouped_pool = ctx.enter_context(tc.tile_pool(name="grouped", bufs=3))
+        result_pool = ctx.enter_context(tc.tile_pool(name="result", bufs=6))
         t_psum = ctx.enter_context(tc.psum_pool(name="t_psum", bufs=T_BANKS))
         o_psum = ctx.enter_context(tc.psum_pool(name="o_psum", bufs=O_BANKS))
-        ctx.enter_context(tc.manual_schedule())
+        ctx.enter_context(tc.manual_schedule(engines={mybir.EngineType.PE, mybir.EngineType.SP}))
 
         token_tiles = [keep.tile([P, HD], BF16, name="tokens%d" % i) for i in range(TOK_TILES)]
         raw = {}
@@ -74,12 +76,12 @@ def tile_attentionlayerdecoder_pa_kernel(
 
         load_tokens(0)
 
-        eps_col = keep.tile([P, 1], F32)
-        nc.vector.memset(eps_col[:], EPS)
         gain_row = keep.tile([P, HD], BF16)
         nc.vector.memset(gain_row[:].bitcast(I32), 0)
         ones = keep.tile([P, P], BF16)
         nc.vector.memset(ones[:], 1.0)
+        eps_col = keep.tile([P, 1], F32)
+        nc.vector.memset(eps_col[:], EPS)
         ident = keep.tile([P, P], F32)
         make_identity(nc, ident[:])
 
@@ -110,9 +112,9 @@ def tile_attentionlayerdecoder_pa_kernel(
                 first += width
 
         def spread(row, everywhere, copy):
-            for first in range(0, row.shape[1], BIAS_COLS):
-                bank = t_psum.tile([P, BIAS_COLS], BF16, tag="bank")
-                for c in range(0, BIAS_COLS, 512):
+            for first in range(0, row.shape[1], SPREAD):
+                bank = t_psum.tile([P, SPREAD], BF16, tag="bank")
+                for c in range(0, SPREAD, 512):
                     nc.tensor.matmul(
                         out=bank[:, c : c + 512],
                         lhsT=ones[:],
@@ -120,68 +122,94 @@ def tile_attentionlayerdecoder_pa_kernel(
                         start=True,
                         stop=True,
                     )
-                copy(out=everywhere[:, first : first + BIAS_COLS], in_=bank[:])
+                copy(out=everywhere[:, first : first + SPREAD], in_=bank[:])
 
         sums = {}
+        offsets = {}
         roots = {}
         rstds = {}
+        x_rows = {}
 
         def square(i):
             squares = rows_pool.tile([P, HD], BF16, tag="squares")
             sums[i] = stats.tile([P, 1], F32, name="sum_sq", tag="sum_sq")
+            cols = slice(0, HALVES if i == 0 else HD)
             nc.scalar.activation(
-                out=squares[:], in_=token_tiles[i][:], func=ACT.Square, accum_out=sums[i][:]
+                out=squares[:, cols], in_=token_tiles[i][:, cols], func=ACT.Square, accum_out=sums[i][:]
             )
+            if i == 0:
+                cols = slice(HALVES, HD)
+                rest = stats.tile([P, 1], F32, tag="sum_rest")
+                nc.vector.scalar_tensor_tensor(
+                    out=squares[:, cols],
+                    in0=token_tiles[i][:, cols],
+                    scalar=1.0,
+                    in1=token_tiles[i][:, cols],
+                    op0=ALU.mult,
+                    op1=ALU.mult,
+                    accum_out=rest[:],
+                )
+                offsets[i] = stats.tile([P, 1], F32, name="offset", tag="offset")
+                nc.vector.tensor_scalar(
+                    out=offsets[i][:], in0=rest[:], scalar1=1.0 / HD, scalar2=EPS, op0=ALU.mult, op1=ALU.add
+                )
 
         def root(i):
             roots[i] = stats.tile([P, 1], F32, name="rms", tag="rms")
             nc.scalar.activation(
-                out=roots[i][:], in_=sums[i][:], func=ACT.Sqrt, scale=1.0 / HD, bias=eps_col[:]
+                out=roots[i][:], in_=sums[i][:], func=ACT.Sqrt, scale=1.0 / HD, bias=offsets.get(i, eps_col)[:]
             )
-
-        x_rows = {}
 
         def invert(i):
             rstds[i] = stats.tile([P, 1], F32, name="rstd", tag="rstd")
             nc.vector.reciprocal(out=rstds[i][:], in_=roots[i][:])
-            x_rows[i] = rows_pool.tile([P, 2, HALVES], BF16, name="x_rows", tag="x_rows")
+            x_rows[i] = rows_pool.tile([P, HD], BF16, name="x_rows", tag="x_rows")
 
-        def normalise(i, us=(0, 1)):
-            for u in us:
-                nc.vector.scalar_tensor_tensor(
-                    out=x_rows[i][:, u, :].rearrange("n (m e) -> n m e", e=2),
-                    in0=token_tiles[i][:].rearrange("n (m u e) -> n m u e", u=2, e=2)[:, :, u, :],
-                    scalar=rstds[i][:, 0:1],
-                    in1=gain_all[:].rearrange("n (m u e) -> n m u e", u=2, e=2)[:, :, u, :],
-                    op0=ALU.mult,
-                    op1=ALU.mult,
-                )
+        def normalise(i, half):
+            cols = slice(half * HALVES, (half + 1) * HALVES)
+            nc.vector.scalar_tensor_tensor(
+                out=x_rows[i][:, cols],
+                in0=token_tiles[i][:, cols],
+                scalar=rstds[i][:, 0:1],
+                in1=gain_all[:, cols],
+                op0=ALU.mult,
+                op1=ALU.mult,
+            )
 
         banks = {}
 
-        def transpose_x(i):
-            words = x_rows[i][:].rearrange("n u k -> n (u k)").bitcast(F32)
+        def transpose_half(key, rows, half, laid_out):
+            words = rows[:].bitcast(F32)
+            bank = t_psum.tile([P, HALF, 2, P], F32, tag="bank")
+            for gg in range(HALF):
+                for u in range(2):
+                    g = half * HALF + gg
+                    if laid_out:
+                        first = (2 * g + u) * P
+                        part = words[:, first : first + P]
+                    else:
+                        part = words[:, 2 * g * P + u : 2 * (g + 1) * P : 2]
+                    nc.tensor.transpose(out=bank[:, gg, u, :], in_=part, identity=ident[:])
+            banks[key + (half,)] = bank
+
+        def transpose_x(i, half):
+            transpose_half(("x", i), x_rows[i], half, False)
+
+        def transpose_w(h):
             for half in range(2):
-                bank = t_psum.tile([P, 2, 2, P], F32, tag="bank")
-                for gg in range(2):
-                    for u in range(2):
-                        first = (u * PASSES + 2 * half + gg) * P
-                        nc.tensor.transpose(
-                            out=bank[:, gg, u, :], in_=words[:, first : first + P], identity=ident[:]
-                        )
-                banks[("x", i, half)] = bank
+                transpose_half(("w", h), perm.get(h, raw[h]), half, h in perm)
 
         grouped_x = {}
 
-        def empty_x(i, copy):
-            grouped_x[i] = rows_pool.tile([P, PASSES, P, PACK], BF16, name="grouped_x", tag="grouped_x", align_bytes=64)
+        def empty_x(i, half, copy):
+            if half == 0:
+                grouped_x[i] = rows_pool.tile([P, PASSES, P, PACK], BF16, name="grouped_x", tag="grouped_x", align_bytes=64)
             words = grouped_x[i][:].rearrange("p g n t -> p (g n t)").bitcast(F32)
             words = words.rearrange("p (g n u) -> p g n u", g=PASSES, u=2)
-            for half in range(2):
-                copy(
-                    out=words[:, 2 * half : 2 * half + 2, :, :],
-                    in_=banks[("x", i, half)][:].rearrange("p g u n -> p g n u"),
-                )
+            copy(
+                out=words[:, half * HALF : (half + 1) * HALF, :, :],
+                in_=banks[("x", i, half)][:].rearrange("p g u n -> p g n u"),
+            )
 
         def quantise_x(i):
             nc.vector.quantize_mx(
@@ -191,49 +219,31 @@ def tile_attentionlayerdecoder_pa_kernel(
             )
 
         def permute(h, copy):
-            perm[h] = perm_pool.tile([P, 2, HALVES], BF16, name="perm_head", tag="perm_head")
+            perm[h] = perm_pool.tile([P, HD], BF16, name="perm_head", tag="perm_head")
             copy(
-                out=perm[h][:].rearrange("o u k -> o (u k)").bitcast(F32).rearrange("o (u m) -> o u m", u=2),
-                in_=raw[h][:].bitcast(F32).rearrange("o (m u) -> o u m", u=2),
+                out=perm[h][:].bitcast(F32).rearrange("o (g u m) -> o g u m", g=PASSES, u=2),
+                in_=raw[h][:].bitcast(F32).rearrange("o (g m u) -> o g u m", g=PASSES, u=2),
             )
-
-        def transpose_w(k):
-            for g in range(PASSES):
-                bank = t_psum.tile([P, 2, UNIT], F32, tag="bank")
-                for r in range(UNIT_HEADS):
-                    h = UNIT_HEADS * k + r
-                    for u in range(2):
-                        if h in perm:
-                            first = (u * PASSES + g) * P
-                            words = perm[h][:].rearrange("o u k -> o (u k)").bitcast(F32)
-                            words = words[:, first : first + P]
-                        else:
-                            words = raw[h][:].bitcast(F32)[:, 2 * g * P + u : 2 * (g + 1) * P : 2]
-                        nc.tensor.transpose(
-                            out=bank[:, u, r * P : (r + 1) * P],
-                            in_=words,
-                            identity=ident[:],
-                        )
-                banks[("w", k, g)] = bank
 
         grouped_w = {}
 
-        def empty_w(k, g, copy):
-            if g % 2 == 0:
-                grouped_w[(k, g // 2)] = grouped_pool.tile([P, 2, UNIT * PACK], BF16, name="grouped_w", tag="grouped_w", align_bytes=64)
-            words = grouped_w[(k, g // 2)][:].rearrange("p g c -> p (g c)").bitcast(F32)
-            words = words.rearrange("p (g o u) -> p g o u", g=2, u=2)
+        def empty_w(h, half, copy):
+            k, r = divmod(h, UNIT_HEADS)
+            if r == 0 and half == 0:
+                grouped_w[k] = grouped_pool.tile([P, PASSES, UNIT * PACK], BF16, name="grouped_w", tag="grouped_w", align_bytes=64)
+            words = grouped_w[k][:].rearrange("p g c -> p (g c)").bitcast(F32)
+            words = words.rearrange("p (g o u) -> p g o u", g=PASSES, u=2)
             copy(
-                out=words[:, g % 2, :, :],
-                in_=banks[("w", k, g)][:].rearrange("p u o -> p o u"),
+                out=words[:, half * HALF : (half + 1) * HALF, r * P : (r + 1) * P, :],
+                in_=banks[("w", h, half)][:].rearrange("p g u o -> p g o u"),
             )
 
         def quantise_w(k, half):
-            g = slice(2 * half, 2 * half + 2)
+            g = slice(half * HALF, (half + 1) * HALF)
             nc.vector.quantize_mx(
                 out=w_codes[k][:, g, :].rearrange("p g o -> p (g o)").bitcast(FP8X4),
                 scales=w_scales[k][:, g, :].rearrange("p g o -> p (g o)"),
-                in_=grouped_w[(k, half)][:].rearrange("p g c -> p (g c)"),
+                in_=grouped_w[k][:, g, :].rearrange("p g c -> p (g c)"),
             )
 
         def multiply(k, pair, tiles=(0, 1)):
@@ -273,95 +283,75 @@ def tile_attentionlayerdecoder_pa_kernel(
         V = nc.vector.tensor_copy
         S = nc.scalar.copy
 
+        def load_heads(first, last):
+            for h in range(first, min(last, n_heads)):
+                load_head(h)
+
         load_gain()
+        load_head(0)
         load_tokens(1)
-        for h in range(6):
-            load_head(h)
-        load_biases()
+        load_heads(1, 6)
         load_tokens(2)
-        load_head(6)
-        load_head(7)
+        load_heads(6, 10)
         load_tokens(3)
-        for h in range(8, RAW_BUFS):
-            load_head(h)
+        load_heads(10, RAW_BUFS)
+        load_biases()
 
-        NS = 6
+        def prepare_x(i):
+            square(i)
+            root(i)
+            invert(i)
+            for half in range(2):
+                normalise(i, half)
+
+        def pack_x(i):
+            for half in range(2):
+                transpose_x(i, half)
+                empty_x(i, half, S)
+            quantise_x(i)
+
+        def prepare_w(k):
+            for h in range(UNIT_HEADS * k, UNIT_HEADS * (k + 1)):
+                if h >= FIRST_LAID_OUT:
+                    permute(h, S if h % 2 == 0 else V)
+                transpose_w(h)
+                for half in range(2):
+                    empty_w(h, half, S)
+            load_heads(RAW_BUFS + UNIT_HEADS * k, RAW_BUFS + UNIT_HEADS * (k + 1))
+            for half in range(2):
+                quantise_w(k, half)
+
+        waiting = sorted(
+            ((k, pair) for k in range(UNITS) for pair in range(2)), key=lambda m: m[0] + LAG * m[1]
+        )
+        to_finish = []
+
+        def multiply_next(count, packed_pairs, units):
+            ready = [m for m in waiting if m[0] < units and m[1] < packed_pairs]
+            for m in ready[:count]:
+                waiting.remove(m)
+                multiply(*m)
+                to_finish.append(m)
+                if len(to_finish) > 1:
+                    finish(*to_finish.pop(0), nc.sync)
+
         spread(gain_row, gain_all, V)
-        square(0)
-        root(0)
-        square(1)
-        root(1)
-        transpose_w(0)
-        invert(0)
-        normalise(0)
-        empty_w(0, 0, S)
-        empty_w(0, 1, S)
-        transpose_x(0)
-        invert(1)
-        normalise(1)
-        empty_x(0, S)
-        transpose_w(1)
-        empty_w(0, 2, S)
-        empty_w(0, 3, S)
-        quantise_x(0)
-        quantise_w(0, 0)
-        quantise_w(0, 1)
-        transpose_x(1)
-        empty_x(1, S)
-        multiply(0, 0, (0,))
-        empty_w(1, 0, V)
-        empty_w(1, 1, S)
-        empty_w(1, 2, V)
-        quantise_x(1)
-        empty_w(1, 3, S)
-
-        xs = {0: ["sq2"], 1: ["nm2", "sq3"], 2: ["tx2", "nm3"], 3: ["qx2", "tx3"], 4: ["qx3"]}
-        owed = []
-        done = []
-        for k in range(UNITS + 1):
-            if k + 2 < UNITS:
-                transpose_w(k + 2)
-            if k < UNITS:
-                multiply(k, 0, (0, 1) if k else (1,))
-            for kk, pair in done:
-                finish(kk, pair, nc.gpsimd if k < 9 else nc.sync)
-            done = [(k, 0)] if k < UNITS else []
-            owed.append(k)
-            if k + 2 < UNITS:
-                empty_w(k + 2, 0, S)
-                empty_w(k + 2, 1, S)
-            for r in range(UNIT_HEADS):
-                h = UNIT_HEADS * (k + 3) + r
-                if UNIT_HEADS * NS <= h < len(head_rows):
-                    permute(h, V if r == 0 or k < 7 else S)
-                if k + 1 < UNITS:
-                    quantise_w(k + 1, r)
-            if k + 2 < UNITS:
-                empty_w(k + 2, 2, S)
-                empty_w(k + 2, 3, V if k < 0 else S)
-            for st in xs.get(k, []):
-                i = int(st[2])
-                if st[:2] == "sq":
-                    square(i)
-                    root(i)
-                if st[:2] == "nm":
-                    invert(i)
-                    normalise(i)
-                if st[:2] == "tx":
-                    transpose_x(i)
-                    empty_x(i, S)
-                if st[:2] == "qx":
-                    quantise_x(i)
-            if k >= 5:
-                n = 2 if k < UNITS else len(owed)
-                for kk in owed[:n]:
-                    if kk < UNITS:
-                        multiply(kk, 1)
-                        done.append((kk, 1))
-                owed = owed[n:]
-            h = RAW_BUFS + UNIT_HEADS * k
-            for r in range(UNIT_HEADS):
-                if h + r < len(head_rows):
-                    load_head(h + r)
-        for kk, pair in done:
-            finish(kk, pair, nc.sync)
+        prepare_x(0)
+        for k in range(UNITS):
+            prepare_w(k)
+            if k == 0:
+                prepare_x(1)
+            if k == 1:
+                pack_x(0)
+                pack_x(1)
+            if k in (2, 3):
+                prepare_x(k)
+            if k == 5:
+                pack_x(2)
+                pack_x(3)
+            if k >= 3:
+                multiply_next(1 if k < 5 else 2, 1 if k < 5 else 2, k - 1)
+        for units in range(UNITS - 2, UNITS + 1):
+            multiply_next(len(waiting), 2, units)
+        for m in to_finish:
+            finish(*m, nc.sync)

@@ -30,8 +30,10 @@ PERM_BUFS = 5
 T_BANKS = 5
 O_BANKS = 3
 SPREAD = 1024
+SCALAR_COLS = (HD // 2, HD, 0, HD)
 LAG = 5
 FIRST_LAID_OUT = 14
+FIRST_X_LAID_OUT = 2
 
 FLOPS = 2 * N_TOK * OUT * HD
 
@@ -132,27 +134,30 @@ def tile_attentionlayerdecoder_pa_kernel(
 
         def square(i):
             squares = rows_pool.tile([P, HD], BF16, tag="squares")
-            sums[i] = stats.tile([P, 1], F32, name="sum_sq", tag="sum_sq")
-            cols = slice(0, HALVES if i == 0 else HD)
-            nc.scalar.activation(
-                out=squares[:, cols], in_=token_tiles[i][:, cols], func=ACT.Square, accum_out=sums[i][:]
-            )
-            if i == 0:
-                cols = slice(HALVES, HD)
+            split = SCALAR_COLS[i]
+            if split > 0:
+                sums[i] = stats.tile([P, 1], F32, name="sum_sq", tag="sum_sq")
+                nc.scalar.activation(
+                    out=squares[:, :split], in_=token_tiles[i][:, :split], func=ACT.Square, accum_out=sums[i][:]
+                )
+            if split < HD:
                 rest = stats.tile([P, 1], F32, tag="sum_rest")
                 nc.vector.scalar_tensor_tensor(
-                    out=squares[:, cols],
-                    in0=token_tiles[i][:, cols],
+                    out=squares[:, split:],
+                    in0=token_tiles[i][:, split:],
                     scalar=1.0,
-                    in1=token_tiles[i][:, cols],
+                    in1=token_tiles[i][:, split:],
                     op0=ALU.mult,
                     op1=ALU.mult,
                     accum_out=rest[:],
                 )
-                offsets[i] = stats.tile([P, 1], F32, name="offset", tag="offset")
-                nc.vector.tensor_scalar(
-                    out=offsets[i][:], in0=rest[:], scalar1=1.0 / HD, scalar2=EPS, op0=ALU.mult, op1=ALU.add
-                )
+                if split > 0:
+                    offsets[i] = stats.tile([P, 1], F32, name="offset", tag="offset")
+                    nc.vector.tensor_scalar(
+                        out=offsets[i][:], in0=rest[:], scalar1=1.0 / HD, scalar2=EPS, op0=ALU.mult, op1=ALU.add
+                    )
+                else:
+                    sums[i] = rest
 
         def root(i):
             roots[i] = stats.tile([P, 1], F32, name="rms", tag="rms")
@@ -165,16 +170,28 @@ def tile_attentionlayerdecoder_pa_kernel(
             nc.vector.reciprocal(out=rstds[i][:], in_=roots[i][:])
             x_rows[i] = rows_pool.tile([P, HD], BF16, name="x_rows", tag="x_rows")
 
+        def words_of(row, u):
+            return row.rearrange("n (m u e) -> n m u e", u=2, e=2)[:, :, u, :]
+
+        def u_cols(half, u):
+            first = u * HALVES + half * HALVES // 2
+            return slice(first, first + HALVES // 2)
+
         def normalise(i, half):
             cols = slice(half * HALVES, (half + 1) * HALVES)
-            nc.vector.scalar_tensor_tensor(
-                out=x_rows[i][:, cols],
-                in0=token_tiles[i][:, cols],
-                scalar=rstds[i][:, 0:1],
-                in1=gain_all[:, cols],
-                op0=ALU.mult,
-                op1=ALU.mult,
-            )
+            pieces = [(cols, token_tiles[i][:, cols], gain_all[:, cols])]
+            if i >= FIRST_X_LAID_OUT:
+                pieces = [
+                    (u_cols(half, u), words_of(token_tiles[i][:, cols], u), words_of(gain_all[:, cols], u))
+                    for u in range(2)
+                ]
+            for out_cols, t, gain in pieces:
+                out = x_rows[i][:, out_cols]
+                if i >= FIRST_X_LAID_OUT:
+                    out = out.rearrange("n (m e) -> n m e", e=2)
+                nc.vector.scalar_tensor_tensor(
+                    out=out, in0=t, scalar=rstds[i][:, 0:1], in1=gain, op0=ALU.mult, op1=ALU.mult
+                )
 
         banks = {}
 
@@ -185,7 +202,7 @@ def tile_attentionlayerdecoder_pa_kernel(
                 for u in range(2):
                     g = half * HALF + gg
                     if laid_out:
-                        first = (2 * g + u) * P
+                        first = (u * PASSES + g) * P
                         part = words[:, first : first + P]
                     else:
                         part = words[:, 2 * g * P + u : 2 * (g + 1) * P : 2]
@@ -193,7 +210,7 @@ def tile_attentionlayerdecoder_pa_kernel(
             banks[key + (half,)] = bank
 
         def transpose_x(i, half):
-            transpose_half(("x", i), x_rows[i], half, False)
+            transpose_half(("x", i), x_rows[i], half, i >= FIRST_X_LAID_OUT)
 
         def transpose_w(h):
             for half in range(2):
@@ -221,8 +238,8 @@ def tile_attentionlayerdecoder_pa_kernel(
         def permute(h, copy):
             perm[h] = perm_pool.tile([P, HD], BF16, name="perm_head", tag="perm_head")
             copy(
-                out=perm[h][:].bitcast(F32).rearrange("o (g u m) -> o g u m", g=PASSES, u=2),
-                in_=raw[h][:].bitcast(F32).rearrange("o (g m u) -> o g u m", g=PASSES, u=2),
+                out=perm[h][:].bitcast(F32).rearrange("o (u m) -> o u m", u=2),
+                in_=raw[h][:].bitcast(F32).rearrange("o (m u) -> o u m", u=2),
             )
 
         grouped_w = {}
@@ -337,10 +354,9 @@ def tile_attentionlayerdecoder_pa_kernel(
 
         spread(gain_row, gain_all, V)
         prepare_x(0)
+        prepare_x(1)
         for k in range(UNITS):
             prepare_w(k)
-            if k == 0:
-                prepare_x(1)
             if k == 1:
                 pack_x(0)
                 pack_x(1)

from contextlib import ExitStack

import concourse.mybir as mybir
from concourse.masks import make_identity

F32 = mybir.dt.float32
BF16 = mybir.dt.bfloat16
I32 = mybir.dt.int32
U32 = mybir.dt.uint32
U8 = mybir.dt.uint8
FP8X4 = mybir.dt.float8_e4m3fn_x4
ACT = mybir.ActivationFunctionType
ALU = mybir.AluOpType

P = 128
PACK = 4
N_TOK = 512
HD = 2048
PASSES = HD // (P * PACK)
HALF = PASSES // 2
TOK_TILES = N_TOK // P
HALVES = HD // 2
UNIT_HEADS = 2
UNIT = UNIT_HEADS * P
UNITS = 12
OUT = UNITS * UNIT
EPS = 2.0 ** -23
RAW_BUFS = 12
PERM_BUFS = 5
T_BANKS = 5
O_BANKS = 3
SPREAD = 1024
SCALAR_COLS = (HD // 2, HD, 0, HD)
LAG = 5
FIRST_LAID_OUT = 14
FIRST_X_LAID_OUT = 2

FLOPS = 2 * N_TOK * OUT * HD


def tile_attentionlayerdecoder_pa_kernel(
    tc, tokens, norm_w, Wq, bq, Wk, bk, Wv, bv, out_0, out_1, out_2
):
    nc = tc.nc
    token_rows = tokens.rearrange("b (p i) k -> (b p) i k", i=TOK_TILES)

    head_rows = []
    head_out = []
    for w, out in ((Wq, out_0), (Wk, out_1), (Wv, out_2)):
        for h in range(w.shape[0] // P):
            head_rows.append(w[h * P : (h + 1) * P, :])
            head_out.append((out.rearrange("b h n d -> (b h) n d"), h))
    n_heads = len(head_rows)

    with ExitStack() as ctx:
        keep = ctx.enter_context(tc.tile_pool(name="keep", bufs=1))
        raw_pool = ctx.enter_context(tc.tile_pool(name="raw", bufs=RAW_BUFS))
        perm_pool = ctx.enter_context(tc.tile_pool(name="perm", bufs=PERM_BUFS))
        stats = ctx.enter_context(tc.tile_pool(name="stats", bufs=TOK_TILES))
        rows_pool = ctx.enter_context(tc.tile_pool(name="rows", bufs=2))
        grouped_pool = ctx.enter_context(tc.tile_pool(name="grouped", bufs=3))
        result_pool = ctx.enter_context(tc.tile_pool(name="result", bufs=6))
        t_psum = ctx.enter_context(tc.psum_pool(name="t_psum", bufs=T_BANKS))
        o_psum = ctx.enter_context(tc.psum_pool(name="o_psum", bufs=O_BANKS))
        ctx.enter_context(tc.manual_schedule(engines={mybir.EngineType.PE, mybir.EngineType.SP}))

        token_tiles = [keep.tile([P, HD], BF16, name="tokens%d" % i) for i in range(TOK_TILES)]
        raw = {}
        perm = {}

        def load_tokens(i):
            nc.sync.dma_start(out=token_tiles[i][:], in_=token_rows[:, i, :])

        def load_head(h):
            tile = raw_pool.tile([P, HD], BF16, name="raw_head", tag="raw_head")
            nc.sync.dma_start(out=tile[:], in_=head_rows[h])
            raw[h] = tile

        load_tokens(0)

        gain_row = keep.tile([P, HD], BF16)
        nc.vector.memset(gain_row[:].bitcast(I32), 0)
        ones = keep.tile([P, P], BF16)
        nc.vector.memset(ones[:], 1.0)
        eps_col = keep.tile([P, 1], F32)
        nc.vector.memset(eps_col[:], EPS)
        ident = keep.tile([P, P], F32)
        make_identity(nc, ident[:])

        gain_all = keep.tile([P, HD], BF16)
        bias_all = keep.tile([P, OUT], BF16)
        x_codes = keep.tile([P, TOK_TILES, PASSES, P], U32, align_bytes=64)
        x_scales = keep.tile([P, TOK_TILES, PASSES, P], U8, align_bytes=64)
        w_codes = [
            keep.tile([P, PASSES, UNIT], U32, name="w_codes%d" % k, align_bytes=64)
            for k in range(UNITS)
        ]
        w_scales = [
            keep.tile([P, PASSES, UNIT], U8, name="w_scales%d" % k, align_bytes=64)
            for k in range(UNITS)
        ]

        warm = keep.tile([P, 1], F32)
        nc.scalar.activation(out=warm[:], in_=eps_col[:], func=ACT.Sqrt)

        def load_gain():
            nc.sync.dma_start(out=gain_row[0:1, :], in_=norm_w.rearrange("(o k) -> o k", o=1))

        def load_biases():
            first = 0
            for bias in (bq, bk, bv):
                width = bias.shape[0]
                nc.sync.dma_start(out=bias_all[:, first : first + width], in_=bias.partition_broadcast(P))
                first += width

        def spread(row, everywhere, copy):
            for first in range(0, row.shape[1], SPREAD):
                bank = t_psum.tile([P, SPREAD], BF16, tag="bank")
                for c in range(0, SPREAD, 512):
                    nc.tensor.matmul(
                        out=bank[:, c : c + 512],
                        lhsT=ones[:],
                        rhs=row[:, first + c : first + c + 512],
                        start=True,
                        stop=True,
                    )
                copy(out=everywhere[:, first : first + SPREAD], in_=bank[:])

        sums = {}
        offsets = {}
        roots = {}
        rstds = {}
        x_rows = {}

        def square(i):
            squares = rows_pool.tile([P, HD], BF16, tag="squares")
            split = SCALAR_COLS[i]
            if split > 0:
                sums[i] = stats.tile([P, 1], F32, name="sum_sq", tag="sum_sq")
                nc.scalar.activation(
                    out=squares[:, :split], in_=token_tiles[i][:, :split], func=ACT.Square, accum_out=sums[i][:]
                )
            if split < HD:
                rest = stats.tile([P, 1], F32, tag="sum_rest")
                nc.vector.scalar_tensor_tensor(
                    out=squares[:, split:],
                    in0=token_tiles[i][:, split:],
                    scalar=1.0,
                    in1=token_tiles[i][:, split:],
                    op0=ALU.mult,
                    op1=ALU.mult,
                    accum_out=rest[:],
                )
                if split > 0:
                    offsets[i] = stats.tile([P, 1], F32, name="offset", tag="offset")
                    nc.vector.tensor_scalar(
                        out=offsets[i][:], in0=rest[:], scalar1=1.0 / HD, scalar2=EPS, op0=ALU.mult, op1=ALU.add
                    )
                else:
                    sums[i] = rest

        def root(i):
            roots[i] = stats.tile([P, 1], F32, name="rms", tag="rms")
            nc.scalar.activation(
                out=roots[i][:], in_=sums[i][:], func=ACT.Sqrt, scale=1.0 / HD, bias=offsets.get(i, eps_col)[:]
            )

        def invert(i):
            rstds[i] = stats.tile([P, 1], F32, name="rstd", tag="rstd")
            nc.vector.reciprocal(out=rstds[i][:], in_=roots[i][:])
            x_rows[i] = rows_pool.tile([P, HD], BF16, name="x_rows", tag="x_rows")

        def words_of(row, u):
            return row.rearrange("n (m u e) -> n m u e", u=2, e=2)[:, :, u, :]

        def u_cols(half, u):
            first = u * HALVES + half * HALVES // 2
            return slice(first, first + HALVES // 2)

        def normalise(i, half):
            cols = slice(half * HALVES, (half + 1) * HALVES)
            pieces = [(cols, token_tiles[i][:, cols], gain_all[:, cols])]
            if i >= FIRST_X_LAID_OUT:
                pieces = [
                    (u_cols(half, u), words_of(token_tiles[i][:, cols], u), words_of(gain_all[:, cols], u))
                    for u in range(2)
                ]
            for out_cols, t, gain in pieces:
                out = x_rows[i][:, out_cols]
                if i >= FIRST_X_LAID_OUT:
                    out = out.rearrange("n (m e) -> n m e", e=2)
                nc.vector.scalar_tensor_tensor(
                    out=out, in0=t, scalar=rstds[i][:, 0:1], in1=gain, op0=ALU.mult, op1=ALU.mult
                )

        banks = {}

        def transpose_half(key, rows, half, laid_out):
            words = rows[:].bitcast(F32)
            bank = t_psum.tile([P, HALF, 2, P], F32, tag="bank")
            for gg in range(HALF):
                for u in range(2):
                    g = half * HALF + gg
                    if laid_out:
                        first = (u * PASSES + g) * P
                        part = words[:, first : first + P]
                    else:
                        part = words[:, 2 * g * P + u : 2 * (g + 1) * P : 2]
                    nc.tensor.transpose(out=bank[:, gg, u, :], in_=part, identity=ident[:])
            banks[key + (half,)] = bank

        def transpose_x(i, half):
            transpose_half(("x", i), x_rows[i], half, i >= FIRST_X_LAID_OUT)

        def transpose_w(h):
            for half in range(2):
                transpose_half(("w", h), perm.get(h, raw[h]), half, h in perm)

        grouped_x = {}

        def empty_x(i, half, copy):
            if half == 0:
                grouped_x[i] = rows_pool.tile([P, PASSES, P, PACK], BF16, name="grouped_x", tag="grouped_x", align_bytes=64)
            words = grouped_x[i][:].rearrange("p g n t -> p (g n t)").bitcast(F32)
            words = words.rearrange("p (g n u) -> p g n u", g=PASSES, u=2)
            copy(
                out=words[:, half * HALF : (half + 1) * HALF, :, :],
                in_=banks[("x", i, half)][:].rearrange("p g u n -> p g n u"),
            )

        def quantise_x(i):
            nc.vector.quantize_mx(
                out=x_codes[:, i, :, :].rearrange("p g n -> p (g n)").bitcast(FP8X4),
                scales=x_scales[:, i, :, :].rearrange("p g n -> p (g n)"),
                in_=grouped_x[i][:].rearrange("p g n t -> p (g n t)"),
            )

        def permute(h, copy):
            perm[h] = perm_pool.tile([P, HD], BF16, name="perm_head", tag="perm_head")
            copy(
                out=perm[h][:].bitcast(F32).rearrange("o (u m) -> o u m", u=2),
                in_=raw[h][:].bitcast(F32).rearrange("o (m u) -> o u m", u=2),
            )

        grouped_w = {}

        def empty_w(h, half, copy):
            k, r = divmod(h, UNIT_HEADS)
            if r == 0 and half == 0:
                grouped_w[k] = grouped_pool.tile([P, PASSES, UNIT * PACK], BF16, name="grouped_w", tag="grouped_w", align_bytes=64)
            words = grouped_w[k][:].rearrange("p g c -> p (g c)").bitcast(F32)
            words = words.rearrange("p (g o u) -> p g o u", g=PASSES, u=2)
            copy(
                out=words[:, half * HALF : (half + 1) * HALF, r * P : (r + 1) * P, :],
                in_=banks[("w", h, half)][:].rearrange("p g u o -> p g o u"),
            )

        def quantise_w(k, half):
            g = slice(half * HALF, (half + 1) * HALF)
            nc.vector.quantize_mx(
                out=w_codes[k][:, g, :].rearrange("p g o -> p (g o)").bitcast(FP8X4),
                scales=w_scales[k][:, g, :].rearrange("p g o -> p (g o)"),
                in_=grouped_w[k][:, g, :].rearrange("p g c -> p (g c)"),
            )

        def multiply(k, pair, tiles=(0, 1)):
            if 0 in tiles:
                banks[("o", k, pair)] = o_psum.tile([P, 2, UNIT], F32, name="out_bank", tag="out")
            bank = banks[("o", k, pair)]
            for ii in tiles:
                i = 2 * pair + ii
                for g in range(PASSES):
                    nc.tensor.matmul_mx(
                        out=bank[:, ii, :],
                        lhsT=x_codes[:, i, g, :].bitcast(FP8X4),
                        lhsT_scale=x_scales[:, i, g, :],
                        rhs=w_codes[k][:, g, :].bitcast(FP8X4),
                        rhs_scale=w_scales[k][:, g, :],
                        start=(g == 0),
                        stop=(g == PASSES - 1),
                    )

        def finish(k, pair, queue):
            result = result_pool.tile([P, UNIT_HEADS, 2, P], F32, tag="result")
            bias = bias_all[:, k * UNIT : (k + 1) * UNIT].rearrange("p (h o d) -> p h o d", h=UNIT_HEADS, o=1)
            nc.vector.tensor_tensor(
                out=result[:],
                in0=banks[("o", k, pair)][:].rearrange("p i (h d) -> p h i d", h=UNIT_HEADS),
                in1=bias.to_broadcast([P, UNIT_HEADS, 2, P]),
                op=ALU.add,
            )
            out, h = head_out[UNIT_HEADS * k]
            queue.dma_start(
                out=out[h : h + UNIT_HEADS, :, :].rearrange("h (p i) d -> p h i d", i=TOK_TILES)[
                    :, :, 2 * pair : 2 * pair + 2, :
                ],
                in_=result[:],
            )

        V = nc.vector.tensor_copy
        S = nc.scalar.copy

        def load_heads(first, last):
            for h in range(first, min(last, n_heads)):
                load_head(h)

        load_gain()
        load_head(0)
        load_tokens(1)
        load_heads(1, 6)
        load_tokens(2)
        load_heads(6, 10)
        load_tokens(3)
        load_heads(10, RAW_BUFS)
        load_biases()

        def prepare_x(i):
            square(i)
            root(i)
            invert(i)
            for half in range(2):
                normalise(i, half)

        def pack_x(i):
            for half in range(2):
                transpose_x(i, half)
                empty_x(i, half, S)
            quantise_x(i)

        def prepare_w(k):
            for h in range(UNIT_HEADS * k, UNIT_HEADS * (k + 1)):
                if h >= FIRST_LAID_OUT:
                    permute(h, S if h % 2 == 0 else V)
                transpose_w(h)
                for half in range(2):
                    empty_w(h, half, S)
            load_heads(RAW_BUFS + UNIT_HEADS * k, RAW_BUFS + UNIT_HEADS * (k + 1))
            for half in range(2):
                quantise_w(k, half)

        waiting = sorted(
            ((k, pair) for k in range(UNITS) for pair in range(2)), key=lambda m: m[0] + LAG * m[1]
        )
        to_finish = []

        def multiply_next(count, packed_pairs, units):
            ready = [m for m in waiting if m[0] < units and m[1] < packed_pairs]
            for m in ready[:count]:
                waiting.remove(m)
                multiply(*m)
                to_finish.append(m)
                if len(to_finish) > 1:
                    finish(*to_finish.pop(0), nc.sync)

        spread(gain_row, gain_all, V)
        prepare_x(0)
        prepare_x(1)
        for k in range(UNITS):
            prepare_w(k)
            if k == 1:
                pack_x(0)
                pack_x(1)
            if k in (2, 3):
                prepare_x(k)
            if k == 5:
                pack_x(2)
                pack_x(3)
            if k >= 3:
                multiply_next(1 if k < 5 else 2, 1 if k < 5 else 2, k - 1)
        for units in range(UNITS - 2, UNITS + 1):
            multiply_next(len(waiting), 2, units)
        for m in to_finish:
            finish(*m, nc.sync)
